import numpy as np
import ml_dtypes


def mxq(x, axis, fmt="e4m3"):
    dtype, down = {"e4m3": (ml_dtypes.float8_e4m3fn, 7), "e5m2": (ml_dtypes.float8_e5m2, 14)}[fmt]
    v = np.moveaxis(np.asarray(x, np.float32).astype(ml_dtypes.bfloat16).astype(np.float64), axis, -1)
    blocks = v.reshape(v.shape[:-1] + (-1, 32))
    amax = np.abs(blocks).max(-1, keepdims=True)
    byte = np.maximum(np.where(amax > 0, np.frexp(amax)[1] - 1 + 127, 0) - down, 1)
    scale = np.exp2(byte - 127.0)
    codes = (blocks / scale).astype(np.float32).astype(dtype).astype(np.float64)
    return np.moveaxis((codes * scale).reshape(v.shape), -1, axis)


WIDE = False


def mx_kscale(k):
    if not WIDE:
        return np.ones(k)
    levels = np.array([10, -10, 5, -5, 0])
    a = np.random.permutation(np.resize(levels, k // 512 * 4)).reshape(k // 512, 4)
    idx = np.arange(k)
    return np.exp2(a[idx // 512, idx % 128 // 32])


BF16 = ml_dtypes.bfloat16


def bf(x):
    return np.asarray(x, np.float32).astype(BF16)


def f64(x):
    return np.asarray(x).astype(np.float64)


E2M1 = np.array([0.0, 0.5, 1.0, 1.5, 2.0, 3.0, 4.0, 6.0, -0.0, -0.5, -1.0, -1.5, -2.0, -3.0, -4.0, -6.0])


def pack_weight(w, fmt):
    k, n = w.shape
    w = f64(bf(w)).reshape(k // 32, 32, n)
    amax = np.abs(w).max(1)
    if fmt == "e4m3":
        byte = np.frexp(amax)[1] - 1 + 127 - 7
    else:
        mant, ex = np.frexp(amax / 6.0)
        byte = np.where(mant > 0.5, ex, ex - 1) + 127
    byte = np.clip(np.where(amax > 0, byte, 1), 1, 254)
    scaled = (w * np.exp2(127.0 - byte)[:, None, :]).reshape(k, n).astype(np.float32)
    by_word = np.ascontiguousarray(scaled.reshape(k // 512, 128, 4, n).transpose(0, 1, 3, 2))
    if fmt == "e4m3":
        words = by_word.astype(ml_dtypes.float8_e4m3fn).view(np.uint8)
    else:
        c = by_word.astype(ml_dtypes.float4_e2m1fn).view(np.uint8) & 0xF
        words = c[..., 0::2] | (c[..., 1::2] << 4)
    return np.ascontiguousarray(words), np.ascontiguousarray(byte.astype(np.uint8).reshape(k // 512, 16, n))


def unpack_weight(words, scales, fmt):
    g, p, n, _ = words.shape
    if fmt == "e4m3":
        vals = np.ascontiguousarray(words).view(ml_dtypes.float8_e4m3fn).astype(np.float64)
    else:
        nib = np.empty((g, p, n, 4), np.uint8)
        nib[..., 0::2] = words & 0xF
        nib[..., 1::2] = words >> 4
        vals = E2M1[nib]
    vals = vals * np.repeat(np.exp2(scales.astype(np.float64) - 127.0), 8, axis=1)[..., None]
    return vals.transpose(0, 1, 3, 2).reshape(g * 512, n)


B, S, D, H, DK = 2, 64, 16384, 16, 64
E = H * DK
FMT = "e4m3"


def apply_rope(v, sin, cos):
    v_rot = np.stack([-v[..., 1::2], v[..., ::2]], axis=-1).reshape(v.shape)
    return v * cos + v_rot * sin


def setup_inputs():
    s = mx_kscale(D)
    x = bf(np.random.standard_normal((B, S, D)) * s)
    wq = np.random.standard_normal((E, D)) / np.sqrt(D) / s
    wk = np.random.standard_normal((E, D)) / np.sqrt(D) / s
    q_words, q_scales = pack_weight(np.ascontiguousarray(wq.T), FMT)
    k_words, k_scales = pack_weight(np.ascontiguousarray(wk.T), FMT)
    return {"x": x,
            "W_q_words": q_words, "W_q_scales": q_scales,
            "W_k_words": k_words, "W_k_scales": k_scales}


def reference(x, W_q_words, W_q_scales, W_k_words, W_k_scales):
    pos = np.arange(S, dtype=np.float64)
    inv_freq = 1.0 / (10000.0 ** (np.arange(0, DK, 2, dtype=np.float64) / DK))
    ang = pos[:, None] * inv_freq
    sin = np.repeat(np.sin(ang), 2, axis=-1)[None, None]
    cos = np.repeat(np.cos(ang), 2, axis=-1)[None, None]
    xq = mxq(f64(x), 2, "e4m3")

    def proj(words, scales):
        y = xq @ unpack_weight(words, scales, FMT)
        return y.reshape(B, S, H, DK).transpose(0, 2, 1, 3)

    return apply_rope(proj(W_q_words, W_q_scales), sin, cos), apply_rope(proj(W_k_words, W_k_scales), sin, cos)

@@ -1,0 +1,218 @@
+import math
+from contextlib import ExitStack
+
+import concourse.mybir as mybir
+from concourse.masks import make_identity
+
+F32 = mybir.dt.float32
+BF16 = mybir.dt.bfloat16
+I32 = mybir.dt.int32
+U32 = mybir.dt.uint32
+U8 = mybir.dt.uint8
+FP8X4 = mybir.dt.float8_e4m3fn_x4
+ALU = mybir.AluOpType
+ACT = mybir.ActivationFunctionType
+
+P = 128
+PACK = 4
+K_PASS = P * PACK
+
+BATCH, POSITIONS, D_IN = 2, 64, 16384
+HEADS, HEAD_DIM = 16, 64
+PAIRS = HEAD_DIM // 2
+DOUBLINGS = 5
+assert 2**DOUBLINGS == PAIRS
+D_OUT = HEADS * HEAD_DIM
+ROPE_BASE = 10000.0
+
+GROUPS = D_IN // K_PASS
+BANK_COLS = 512
+BANKS = D_OUT // BANK_COLS
+BANK_HEADS = BANK_COLS // HEAD_DIM
+
+X_CHUNKS = 4
+CHUNK_GROUPS = GROUPS // X_CHUNKS
+BANK_GROUPS = 2
+
+QUADRANT = 32
+QUADRANTS = P // QUADRANT
+SCALE_ROWS = 4
+PLANES = 4
+SLOTS = GROUPS // PLANES
+
+WEIGHT_BUFS = 32
+
+FLOPS = 2 * BATCH * POSITIONS * D_IN * 2 * D_OUT
+
+
+def load_scale_planes(nc, planes, scales):
+    by_row = scales.bitcast(F32).rearrange("(slot i) q n -> q i slot n", i=PLANES)
+    for quadrant in range(QUADRANTS):
+        for r in range(SCALE_ROWS):
+            first = QUADRANT * quadrant + r
+            nc.gpsimd.dma_start(
+                out=planes[first : first + PLANES * SCALE_ROWS : SCALE_ROWS, :, :].bitcast(F32),
+                in_=by_row[SCALE_ROWS * quadrant + r],
+            )
+
+
+def build_rotation_tables(nc, pool):
+    pos_int = pool.tile([P, 1], I32)
+    nc.gpsimd.iota(pos_int[:], pattern=[[1, 1]], base=0, channel_multiplier=1)
+    nc.vector.tensor_single_scalar(
+        out=pos_int[:], in_=pos_int[:], scalar=POSITIONS - 1, op=ALU.bitwise_and
+    )
+    pos_turns = pool.tile([P, 1], F32)
+    nc.vector.tensor_copy(out=pos_turns[:], in_=pos_int[:])
+    nc.vector.tensor_scalar_mul(out=pos_turns[:], in0=pos_turns[:], scalar1=1.0 / (2.0 * math.pi))
+
+    ratio = ROPE_BASE ** (-2.0 / HEAD_DIM)
+    inv_freq = pool.tile([P, PAIRS], F32)
+    nc.vector.memset(inv_freq[:, 0:1], 1.0)
+    for doubling in range(DOUBLINGS):
+        length = 2**doubling
+        nc.vector.tensor_scalar_mul(
+            out=inv_freq[:, length : 2 * length], in0=inv_freq[:, 0:length], scalar1=ratio**length
+        )
+
+    turns = pool.tile([P, 2, PAIRS], F32)
+    for row, phase in enumerate((0.0, 0.25)):
+        nc.vector.tensor_scalar(
+            out=turns[:, row, :],
+            in0=inv_freq[:],
+            scalar1=pos_turns[:, 0:1],
+            scalar2=phase,
+            op0=ALU.mult,
+            op1=ALU.add,
+        )
+    whole_int = pool.tile([P, 2, PAIRS], I32)
+    nc.vector.tensor_copy(out=whole_int[:], in_=turns[:])
+    whole = pool.tile([P, 2, PAIRS], F32)
+    nc.vector.tensor_copy(out=whole[:], in_=whole_int[:])
+    nc.vector.tensor_tensor(out=turns[:], in0=turns[:], in1=whole[:], op=ALU.subtract)
+    nc.vector.tensor_single_scalar(out=whole[:], in_=turns[:], scalar=0.5, op=ALU.is_gt)
+    nc.vector.tensor_tensor(out=turns[:], in0=turns[:], in1=whole[:], op=ALU.subtract)
+    sin_cos = pool.tile([P, 2, PAIRS], F32)
+    nc.scalar.activation(out=sin_cos[:], in_=turns[:], func=ACT.Sin, scale=2.0 * math.pi)
+    neg_sin = pool.tile([P, PAIRS], F32)
+    nc.vector.tensor_scalar_mul(out=neg_sin[:], in0=sin_cos[:, 0, :], scalar1=-1.0)
+    return sin_cos[:, 0, :], sin_cos[:, 1, :], neg_sin[:]
+
+
+def rotate_and_store(nc, pool, bank, first_head, tables, out, queue):
+    sin, cos, neg_sin = tables
+    y = bank[:].rearrange("p (h i two) -> p h i two", h=BANK_HEADS, two=2)
+    by_head = [P, BANK_HEADS, PAIRS]
+    direct = pool.tile([P, BANK_HEADS, PAIRS, 2], F32)
+    nc.vector.tensor_tensor(
+        out=direct[:],
+        in0=y,
+        in1=cos.unsqueeze(1).unsqueeze(3).to_broadcast([P, BANK_HEADS, PAIRS, 2]),
+        op=ALU.mult,
+    )
+    crossed = pool.tile([P, 2, BANK_HEADS, PAIRS], F32)
+    nc.vector.tensor_tensor(
+        out=crossed[:, 0], in0=y[:, :, :, 1], in1=neg_sin.unsqueeze(1).to_broadcast(by_head), op=ALU.mult
+    )
+    nc.vector.tensor_tensor(
+        out=crossed[:, 1], in0=y[:, :, :, 0], in1=sin.unsqueeze(1).to_broadcast(by_head), op=ALU.mult
+    )
+    rotated = pool.tile([P, BANK_HEADS, PAIRS, 2], F32)
+    nc.vector.tensor_tensor(
+        out=rotated[:],
+        in0=direct[:],
+        in1=crossed[:].rearrange("p two h i -> p h i two"),
+        op=ALU.add,
+    )
+    for b in range(BATCH):
+        queue.dma_start(
+            out=out[b, first_head : first_head + BANK_HEADS].rearrange("h s d -> s h d"),
+            in_=rotated[b * POSITIONS : (b + 1) * POSITIONS].rearrange("p h i two -> p h (i two)"),
+        )
+
+
+def tile_optimizedflashattention_pa_k_kernel(
+    tc, x, w_q_words, w_q_scales, w_k_words, w_k_scales, out_q, out_k
+):
+    nc = tc.nc
+    with ExitStack() as ctx:
+        keep = ctx.enter_context(tc.tile_pool(name="keep", bufs=1))
+        stage = ctx.enter_context(tc.tile_pool(name="stage", bufs=3))
+        weights = ctx.enter_context(tc.tile_pool(name="weights", bufs=WEIGHT_BUFS))
+        rope = ctx.enter_context(tc.tile_pool(name="rope", bufs=2))
+        flipped = ctx.enter_context(tc.psum_pool(name="flipped", bufs=4))
+        sums = ctx.enter_context(tc.psum_pool(name="sums", bufs=1))
+
+        x_rows = x.rearrange("b s d -> (b s) d")
+        chunk_cols = CHUNK_GROUPS * K_PASS
+        x_chunks = []
+        for c in range(X_CHUNKS):
+            x_chunk = keep.tile([P, chunk_cols], BF16, name="x_chunk%d" % c)
+            nc.sync.dma_start(out=x_chunk[:], in_=x_rows[:, c * chunk_cols : (c + 1) * chunk_cols])
+            x_chunks.append(x_chunk)
+
+        identity = keep.tile([P, P], F32)
+        make_identity(nc, identity[:])
+        projections = []
+        for name, words, scales, out in (
+            ("q", w_q_words, w_q_scales, out_q),
+            ("k", w_k_words, w_k_scales, out_k),
+        ):
+            planes = keep.tile([P, SLOTS, D_OUT], U8, name="planes_%s" % name, align_bytes=64)
+            nc.vector.memset(planes[:].rearrange("p slot n -> p (slot n)").bitcast(I32), 0)
+            load_scale_planes(nc, planes, scales)
+            projections.append((name, words, planes, out))
+
+        x_codes = keep.tile([P, GROUPS, P], U32, align_bytes=64)
+        x_scales = keep.tile([P, GROUPS, P], U8, align_bytes=64)
+        words_per_group = K_PASS // 2
+        for c in range(X_CHUNKS):
+            x_words = x_chunks[c][:].bitcast(F32)
+            for first in range(0, CHUNK_GROUPS, BANK_GROUPS):
+                x_t = flipped.tile([P, BANK_GROUPS, 2, P], F32)
+                for j in range(BANK_GROUPS):
+                    start_word = (first + j) * words_per_group
+                    for u in range(2):
+                        nc.tensor.transpose(
+                            x_t[:, j, u, :],
+                            x_words[:, start_word + u : start_word + words_per_group : 2],
+                            identity[:],
+                        )
+                grouped = stage.tile([P, BANK_GROUPS, P, PACK], BF16, align_bytes=64)
+                nc.scalar.copy(
+                    out=grouped[:].bitcast(F32), in_=x_t[:].rearrange("p j u token -> p j token u")
+                )
+                g = c * CHUNK_GROUPS + first
+                nc.vector.quantize_mx(
+                    out=x_codes[:, g : g + BANK_GROUPS, :]
+                    .rearrange("p j token -> p (j token)")
+                    .bitcast(FP8X4),
+                    scales=x_scales[:, g : g + BANK_GROUPS, :].rearrange("p j token -> p (j token)"),
+                    in_=grouped[:].rearrange("p j token t -> p (j token t)"),
+                )
+
+        tables = build_rotation_tables(nc, keep)
+
+        for name, words, planes, out in projections:
+            banks = [sums.tile([P, BANK_COLS], F32, name="sum_%s%d" % (name, n)) for n in range(BANKS)]
+            for g in range(GROUPS):
+                w_codes = weights.tile([P, D_OUT], U32, align_bytes=64)
+                nc.sync.dma_start(
+                    out=w_codes[:].bitcast(I32),
+                    in_=words[g].rearrange("p n t -> p (n t)").bitcast(I32),
+                )
+                slot, i = divmod(g, PLANES)
+                for n in range(BANKS):
+                    cols = slice(n * BANK_COLS, (n + 1) * BANK_COLS)
+                    nc.tensor.matmul_mx(
+                        out=banks[n][:],
+                        lhsT=x_codes[:, g, :].bitcast(FP8X4),
+                        lhsT_scale=x_scales[:, g, :],
+                        rhs=w_codes[:, cols].bitcast(FP8X4),
+                        rhs_scale=planes[SCALE_ROWS * i : P, slot, cols],
+                        start=(g == 0),
+                        stop=(g == GROUPS - 1),
+                    )
+            queue = nc.scalar if name == "q" else nc.sync
+            for n in range(BANKS):
+                rotate_and_store(nc, rope, banks[n], n * BANK_HEADS, tables, out, queue)

@@ -40,7 +40,7 @@ SCALE_ROWS = 4
 PLANES = 4
 SLOTS = GROUPS // PLANES
 
-WEIGHT_BUFS = 32
+WEIGHT_BUFS = 7
 
 FLOPS = 2 * BATCH * POSITIONS * D_IN * 2 * D_OUT
 
@@ -131,6 +131,18 @@ def rotate_and_store(nc, pool, bank, first_head, tables, out, queue):
         )
 
 
+def multiply_group(nc, bank, x_codes, x_scales, g, w_codes, w_scales):
+    nc.tensor.matmul_mx(
+        out=bank[:],
+        lhsT=x_codes[:, g, :].bitcast(FP8X4),
+        lhsT_scale=x_scales[:, g, :],
+        rhs=w_codes.bitcast(FP8X4),
+        rhs_scale=w_scales,
+        start=(g == 0),
+        stop=(g == GROUPS - 1),
+    )
+
+
 def tile_optimizedflashattention_pa_k_kernel(
     tc, x, w_q_words, w_q_scales, w_k_words, w_k_scales, out_q, out_k
 ):
@@ -139,6 +151,7 @@ def tile_optimizedflashattention_pa_k_kernel(
         keep = ctx.enter_context(tc.tile_pool(name="keep", bufs=1))
         stage = ctx.enter_context(tc.tile_pool(name="stage", bufs=3))
         weights = ctx.enter_context(tc.tile_pool(name="weights", bufs=WEIGHT_BUFS))
+        halves = ctx.enter_context(tc.tile_pool(name="halves", bufs=2))
         rope = ctx.enter_context(tc.tile_pool(name="rope", bufs=2))
         flipped = ctx.enter_context(tc.psum_pool(name="flipped", bufs=4))
         sums = ctx.enter_context(tc.psum_pool(name="sums", bufs=1))
@@ -194,25 +207,33 @@ def tile_optimizedflashattention_pa_k_kernel(
         tables = build_rotation_tables(nc, keep)
 
         for name, words, planes, out in projections:
-            banks = [sums.tile([P, BANK_COLS], F32, name="sum_%s%d" % (name, n)) for n in range(BANKS)]
-            for g in range(GROUPS):
-                w_codes = weights.tile([P, D_OUT], U32, align_bytes=64)
-                nc.sync.dma_start(
-                    out=w_codes[:].bitcast(I32),
-                    in_=words[g].rearrange("p n t -> p (n t)").bitcast(I32),
-                )
-                slot, i = divmod(g, PLANES)
-                for n in range(BANKS):
-                    cols = slice(n * BANK_COLS, (n + 1) * BANK_COLS)
-                    nc.tensor.matmul_mx(
-                        out=banks[n][:],
-                        lhsT=x_codes[:, g, :].bitcast(FP8X4),
-                        lhsT_scale=x_scales[:, g, :],
-                        rhs=w_codes[:, cols].bitcast(FP8X4),
-                        rhs_scale=planes[SCALE_ROWS * i : P, slot, cols],
-                        start=(g == 0),
-                        stop=(g == GROUPS - 1),
-                    )
             queue = nc.scalar if name == "q" else nc.sync
+            banks = [sums.tile([P, BANK_COLS], F32, name="sum_%s%d" % (name, n)) for n in range(BANKS)]
+            by_block = words.rearrange("(slot i) p n t -> slot p i (n t)", i=PLANES).bitcast(I32)
+            for slot in range(SLOTS - 1):
+                w_block = weights.tile([P, PLANES, D_OUT], U32, align_bytes=64)
+                nc.sync.dma_start(out=w_block[:].bitcast(I32), in_=by_block[slot])
+                for i in range(PLANES):
+                    for n in range(BANKS):
+                        cols = slice(n * BANK_COLS, (n + 1) * BANK_COLS)
+                        multiply_group(
+                            nc, banks[n], x_codes, x_scales, slot * PLANES + i,
+                            w_block[:, i, cols], planes[SCALE_ROWS * i : P, slot, cols],
+                        )
+            slot = SLOTS - 1
+            w_halves = []
             for n in range(BANKS):
+                w_half = halves.tile([P, PLANES, BANK_COLS], U32, align_bytes=64)
+                nc.sync.dma_start(
+                    out=w_half[:].bitcast(I32),
+                    in_=by_block[slot][:, :, n * BANK_COLS : (n + 1) * BANK_COLS],
+                )
+                w_halves.append(w_half)
+            for n in range(BANKS):
+                cols = slice(n * BANK_COLS, (n + 1) * BANK_COLS)
+                for i in range(PLANES):
+                    multiply_group(
+                        nc, banks[n], x_codes, x_scales, slot * PLANES + i,
+                        w_halves[n][:, i, :], planes[SCALE_ROWS * i : P, slot, cols],
+                    )
                 rotate_and_store(nc, rope, banks[n], n * BANK_HEADS, tables, out, queue)

@@ -47,8 +47,8 @@ FLOPS = 2 * BATCH * POSITIONS * D_IN * 2 * D_OUT
 
 def load_scale_planes(nc, planes, scales):
     by_row = scales.bitcast(F32).rearrange("(slot i) q n -> q i slot n", i=PLANES)
-    for quadrant in range(QUADRANTS):
-        for r in range(SCALE_ROWS):
+    for r in range(SCALE_ROWS):
+        for quadrant in range(QUADRANTS):
             first = QUADRANT * quadrant + r
             nc.gpsimd.dma_start(
                 out=planes[first : first + PLANES * SCALE_ROWS : SCALE_ROWS, :, :].bitcast(F32),

@@ -27,8 +27,9 @@ ROPE_BASE = 10000.0
 
 GROUPS = D_IN // K_PASS
 BANK_COLS = 512
-BANKS = D_OUT // BANK_COLS
-BANK_HEADS = BANK_COLS // HEAD_DIM
+
+TILE_COLS = {"q": (512, 512), "k": (512, 256, 128, 128)}
+TILE_BANKS = {"q": (0, 1), "k": (2, 3, 4, 0)}
 
 X_CHUNKS = 4
 CHUNK_GROUPS = GROUPS // X_CHUNKS
@@ -99,25 +100,27 @@ def build_rotation_tables(nc, pool):
     return sin_cos[:, 0, :], sin_cos[:, 1, :], neg_sin[:]
 
 
-def rotate_and_store(nc, pool, bank, first_head, tables, out, queue):
+def rotate_and_store(nc, pool, bank, first_col, cols, tables, out, queues):
     sin, cos, neg_sin = tables
-    y = bank[:].rearrange("p (h i two) -> p h i two", h=BANK_HEADS, two=2)
-    by_head = [P, BANK_HEADS, PAIRS]
-    direct = pool.tile([P, BANK_HEADS, PAIRS, 2], F32)
+    heads = cols // HEAD_DIM
+    first_head = first_col // HEAD_DIM
+    y = bank[:].rearrange("p (h i two) -> p h i two", h=heads, two=2)
+    by_head = [P, heads, PAIRS]
+    direct = pool.tile([P, heads, PAIRS, 2], F32)
     nc.vector.tensor_tensor(
         out=direct[:],
         in0=y,
-        in1=cos.unsqueeze(1).unsqueeze(3).to_broadcast([P, BANK_HEADS, PAIRS, 2]),
+        in1=cos.unsqueeze(1).unsqueeze(3).to_broadcast([P, heads, PAIRS, 2]),
         op=ALU.mult,
     )
-    crossed = pool.tile([P, 2, BANK_HEADS, PAIRS], F32)
+    crossed = pool.tile([P, 2, heads, PAIRS], F32)
     nc.vector.tensor_tensor(
         out=crossed[:, 0], in0=y[:, :, :, 1], in1=neg_sin.unsqueeze(1).to_broadcast(by_head), op=ALU.mult
     )
     nc.vector.tensor_tensor(
         out=crossed[:, 1], in0=y[:, :, :, 0], in1=sin.unsqueeze(1).to_broadcast(by_head), op=ALU.mult
     )
-    rotated = pool.tile([P, BANK_HEADS, PAIRS, 2], F32)
+    rotated = pool.tile([P, heads, PAIRS, 2], F32)
     nc.vector.tensor_tensor(
         out=rotated[:],
         in0=direct[:],
@@ -125,8 +128,8 @@ def rotate_and_store(nc, pool, bank, first_head, tables, out, queue):
         op=ALU.add,
     )
     for b in range(BATCH):
-        queue.dma_start(
-            out=out[b, first_head : first_head + BANK_HEADS].rearrange("h s d -> s h d"),
+        queues[b].dma_start(
+            out=out[b, first_head : first_head + heads].rearrange("h s d -> s h d"),
             in_=rotated[b * POSITIONS : (b + 1) * POSITIONS].rearrange("p h i two -> p h (i two)"),
         )
 
@@ -151,9 +154,9 @@ def tile_optimizedflashattention_pa_k_kernel(
         keep = ctx.enter_context(tc.tile_pool(name="keep", bufs=1))
         stage = ctx.enter_context(tc.tile_pool(name="stage", bufs=3))
         weights = ctx.enter_context(tc.tile_pool(name="weights", bufs=WEIGHT_BUFS))
-        halves = ctx.enter_context(tc.tile_pool(name="halves", bufs=2))
+        parts = ctx.enter_context(tc.tile_pool(name="parts", bufs=1))
         rope = ctx.enter_context(tc.tile_pool(name="rope", bufs=2))
-        flipped = ctx.enter_context(tc.psum_pool(name="flipped", bufs=4))
+        flipped = ctx.enter_context(tc.psum_pool(name="flipped", bufs=3))
         sums = ctx.enter_context(tc.psum_pool(name="sums", bufs=1))
 
         x_rows = x.rearrange("b s d -> (b s) d")
@@ -207,33 +210,39 @@ def tile_optimizedflashattention_pa_k_kernel(
         tables = build_rotation_tables(nc, keep)
 
         for name, words, planes, out in projections:
-            queue = nc.scalar if name == "q" else nc.sync
-            banks = [sums.tile([P, BANK_COLS], F32, name="sum_%s%d" % (name, n)) for n in range(BANKS)]
+            widths = TILE_COLS[name]
+            starts = [sum(widths[:n]) for n in range(len(widths))]
+            spans = [slice(first, first + width) for first, width in zip(starts, widths)]
+            banks = [
+                sums.tile([P, width], F32, name="sum%d" % b) for width, b in zip(widths, TILE_BANKS[name])
+            ]
             by_block = words.rearrange("(slot i) p n t -> slot p i (n t)", i=PLANES).bitcast(I32)
-            for slot in range(SLOTS - 1):
+            whole_blocks = SLOTS if name == "q" else SLOTS - 1
+            for slot in range(whole_blocks):
                 w_block = weights.tile([P, PLANES, D_OUT], U32, align_bytes=64)
                 nc.sync.dma_start(out=w_block[:].bitcast(I32), in_=by_block[slot])
                 for i in range(PLANES):
-                    for n in range(BANKS):
-                        cols = slice(n * BANK_COLS, (n + 1) * BANK_COLS)
+                    for bank, cols in zip(banks, spans):
                         multiply_group(
-                            nc, banks[n], x_codes, x_scales, slot * PLANES + i,
+                            nc, bank, x_codes, x_scales, slot * PLANES + i,
                             w_block[:, i, cols], planes[SCALE_ROWS * i : P, slot, cols],
                         )
-            slot = SLOTS - 1
-            w_halves = []
-            for n in range(BANKS):
-                w_half = halves.tile([P, PLANES, BANK_COLS], U32, align_bytes=64)
-                nc.sync.dma_start(
-                    out=w_half[:].bitcast(I32),
-                    in_=by_block[slot][:, :, n * BANK_COLS : (n + 1) * BANK_COLS],
+            last_parts = []
+            for slot in range(whole_blocks, SLOTS):
+                for n, cols in enumerate(spans):
+                    w_part = parts.tile([P, PLANES, widths[n]], U32, name="w_part%d" % n, align_bytes=64)
+                    nc.sync.dma_start(out=w_part[:].bitcast(I32), in_=by_block[slot][:, :, cols])
+                    last_parts.append((slot, w_part))
+            for n, cols in enumerate(spans):
+                if last_parts:
+                    slot, w_part = last_parts[n]
+                    for i in range(PLANES):
+                        multiply_group(
+                            nc, banks[n], x_codes, x_scales, slot * PLANES + i,
+                            w_part[:, i, :], planes[SCALE_ROWS * i : P, slot, cols],
+                        )
+                at_the_end = name == "k" and n == len(spans) - 1
+                rotate_and_store(
+                    nc, rope, banks[n], starts[n], widths[n], tables, out,
+                    (nc.sync, nc.scalar) if at_the_end else (nc.scalar, nc.scalar),
                 )
-                w_halves.append(w_half)
-            for n in range(BANKS):
-                cols = slice(n * BANK_COLS, (n + 1) * BANK_COLS)
-                for i in range(PLANES):
-                    multiply_group(
-                        nc, banks[n], x_codes, x_scales, slot * PLANES + i,
-                        w_halves[n][:, i, :], planes[SCALE_ROWS * i : P, slot, cols],
-                    )
-                rotate_and_store(nc, rope, banks[n], n * BANK_HEADS, tables, out, queue)

@@ -100,7 +100,7 @@ def build_rotation_tables(nc, pool):
     return sin_cos[:, 0, :], sin_cos[:, 1, :], neg_sin[:]
 
 
-def rotate_and_store(nc, pool, bank, first_col, cols, tables, out, queues):
+def rotate_and_store(nc, pool, keep, name, bank, first_col, cols, tables, out, queues):
     sin, cos, neg_sin = tables
     heads = cols // HEAD_DIM
     first_head = first_col // HEAD_DIM
@@ -120,7 +120,7 @@ def rotate_and_store(nc, pool, bank, first_col, cols, tables, out, queues):
     nc.vector.tensor_tensor(
         out=crossed[:, 1], in0=y[:, :, :, 0], in1=sin.unsqueeze(1).to_broadcast(by_head), op=ALU.mult
     )
-    rotated = pool.tile([P, heads, PAIRS, 2], F32)
+    rotated = keep.tile([P, heads, PAIRS, 2], F32, name="rotated_%s%d" % (name, first_head))
     nc.vector.tensor_tensor(
         out=rotated[:],
         in0=direct[:],
@@ -209,40 +209,41 @@ def tile_optimizedflashattention_pa_k_kernel(
 
         tables = build_rotation_tables(nc, keep)
 
-        for name, words, planes, out in projections:
-            widths = TILE_COLS[name]
-            starts = [sum(widths[:n]) for n in range(len(widths))]
-            spans = [slice(first, first + width) for first, width in zip(starts, widths)]
-            banks = [
-                sums.tile([P, width], F32, name="sum%d" % b) for width, b in zip(widths, TILE_BANKS[name])
-            ]
-            by_block = words.rearrange("(slot i) p n t -> slot p i (n t)", i=PLANES).bitcast(I32)
-            whole_blocks = SLOTS if name == "q" else SLOTS - 1
-            for slot in range(whole_blocks):
-                w_block = weights.tile([P, PLANES, D_OUT], U32, align_bytes=64)
-                nc.sync.dma_start(out=w_block[:].bitcast(I32), in_=by_block[slot])
-                for i in range(PLANES):
-                    for bank, cols in zip(banks, spans):
-                        multiply_group(
-                            nc, bank, x_codes, x_scales, slot * PLANES + i,
-                            w_block[:, i, cols], planes[SCALE_ROWS * i : P, slot, cols],
-                        )
-            last_parts = []
-            for slot in range(whole_blocks, SLOTS):
-                for n, cols in enumerate(spans):
-                    w_part = parts.tile([P, PLANES, widths[n]], U32, name="w_part%d" % n, align_bytes=64)
-                    nc.sync.dma_start(out=w_part[:].bitcast(I32), in_=by_block[slot][:, :, cols])
-                    last_parts.append((slot, w_part))
-            for n, cols in enumerate(spans):
-                if last_parts:
-                    slot, w_part = last_parts[n]
+        with tc.manual_schedule(engines={mybir.EngineType.SP, mybir.EngineType.PE}):
+            for name, words, planes, out in projections:
+                widths = TILE_COLS[name]
+                starts = [sum(widths[:n]) for n in range(len(widths))]
+                spans = [slice(first, first + width) for first, width in zip(starts, widths)]
+                banks = [
+                    sums.tile([P, width], F32, name="sum%d" % b) for width, b in zip(widths, TILE_BANKS[name])
+                ]
+                by_block = words.rearrange("(slot i) p n t -> slot p i (n t)", i=PLANES).bitcast(I32)
+                whole_blocks = SLOTS if name == "q" else SLOTS - 1
+                for slot in range(whole_blocks):
+                    w_block = weights.tile([P, PLANES, D_OUT], U32, align_bytes=64)
+                    nc.sync.dma_start(out=w_block[:].bitcast(I32), in_=by_block[slot])
                     for i in range(PLANES):
-                        multiply_group(
-                            nc, banks[n], x_codes, x_scales, slot * PLANES + i,
-                            w_part[:, i, :], planes[SCALE_ROWS * i : P, slot, cols],
-                        )
-                at_the_end = name == "k" and n == len(spans) - 1
-                rotate_and_store(
-                    nc, rope, banks[n], starts[n], widths[n], tables, out,
-                    (nc.sync, nc.scalar) if at_the_end else (nc.scalar, nc.scalar),
-                )
+                        for bank, cols in zip(banks, spans):
+                            multiply_group(
+                                nc, bank, x_codes, x_scales, slot * PLANES + i,
+                                w_block[:, i, cols], planes[SCALE_ROWS * i : P, slot, cols],
+                            )
+                last_parts = []
+                for slot in range(whole_blocks, SLOTS):
+                    for n, cols in enumerate(spans):
+                        w_part = parts.tile([P, PLANES, widths[n]], U32, name="w_part%d" % n, align_bytes=64)
+                        nc.sync.dma_start(out=w_part[:].bitcast(I32), in_=by_block[slot][:, :, cols])
+                        last_parts.append((slot, w_part))
+                for n, cols in enumerate(spans):
+                    if last_parts:
+                        slot, w_part = last_parts[n]
+                        for i in range(PLANES):
+                            multiply_group(
+                                nc, banks[n], x_codes, x_scales, slot * PLANES + i,
+                                w_part[:, i, :], planes[SCALE_ROWS * i : P, slot, cols],
+                            )
+                    at_the_end = name == "k" and n == len(spans) - 1
+                    rotate_and_store(
+                        nc, rope, keep, name, banks[n], starts[n], widths[n], tables, out,
+                        (nc.sync, nc.scalar) if at_the_end else (nc.scalar, nc.scalar),
+                    )

@@ -28,8 +28,8 @@ ROPE_BASE = 10000.0
 GROUPS = D_IN // K_PASS
 BANK_COLS = 512
 
-TILE_COLS = {"q": (512, 512), "k": (512, 256, 128, 128)}
-TILE_BANKS = {"q": (0, 1), "k": (2, 3, 4, 0)}
+TILE_COLS = {"q": (512, 512), "k": (512, 256, 256)}
+TILE_BANKS = {"q": (0, 1), "k": (2, 3, 4)}
 
 X_CHUNKS = 4
 CHUNK_GROUPS = GROUPS // X_CHUNKS
@@ -100,10 +100,9 @@ def build_rotation_tables(nc, pool):
     return sin_cos[:, 0, :], sin_cos[:, 1, :], neg_sin[:]
 
 
-def rotate_and_store(nc, pool, keep, name, bank, first_col, cols, tables, out, queues):
+def rotate(nc, pool, rotated, bank, tables):
     sin, cos, neg_sin = tables
-    heads = cols // HEAD_DIM
-    first_head = first_col // HEAD_DIM
+    heads = rotated.shape[1]
     y = bank[:].rearrange("p (h i two) -> p h i two", h=heads, two=2)
     by_head = [P, heads, PAIRS]
     direct = pool.tile([P, heads, PAIRS, 2], F32)
@@ -120,13 +119,17 @@ def rotate_and_store(nc, pool, keep, name, bank, first_col, cols, tables, out, q
     nc.vector.tensor_tensor(
         out=crossed[:, 1], in0=y[:, :, :, 0], in1=sin.unsqueeze(1).to_broadcast(by_head), op=ALU.mult
     )
-    rotated = keep.tile([P, heads, PAIRS, 2], F32, name="rotated_%s%d" % (name, first_head))
     nc.vector.tensor_tensor(
         out=rotated[:],
         in0=direct[:],
         in1=crossed[:].rearrange("p two h i -> p h i two"),
         op=ALU.add,
     )
+
+
+def store(queues, rotated, out, first_col):
+    heads = rotated.shape[1]
+    first_head = first_col // HEAD_DIM
     for b in range(BATCH):
         queues[b].dma_start(
             out=out[b, first_head : first_head + heads].rearrange("h s d -> s h d"),
@@ -210,6 +213,7 @@ def tile_optimizedflashattention_pa_k_kernel(
         tables = build_rotation_tables(nc, keep)
 
         with tc.manual_schedule(engines={mybir.EngineType.SP, mybir.EngineType.PE}):
+            waiting = []
             for name, words, planes, out in projections:
                 widths = TILE_COLS[name]
                 starts = [sum(widths[:n]) for n in range(len(widths))]
@@ -234,6 +238,9 @@ def tile_optimizedflashattention_pa_k_kernel(
                         w_part = parts.tile([P, PLANES, widths[n]], U32, name="w_part%d" % n, align_bytes=64)
                         nc.sync.dma_start(out=w_part[:].bitcast(I32), in_=by_block[slot][:, :, cols])
                         last_parts.append((slot, w_part))
+                if name == "k":
+                    for rotated, q_out, first_col in waiting:
+                        store((nc.sync, nc.sync), rotated, q_out, first_col)
                 for n, cols in enumerate(spans):
                     if last_parts:
                         slot, w_part = last_parts[n]
@@ -242,8 +249,12 @@ def tile_optimizedflashattention_pa_k_kernel(
                                 nc, banks[n], x_codes, x_scales, slot * PLANES + i,
                                 w_part[:, i, :], planes[SCALE_ROWS * i : P, slot, cols],
                             )
-                    at_the_end = name == "k" and n == len(spans) - 1
-                    rotate_and_store(
-                        nc, rope, keep, name, banks[n], starts[n], widths[n], tables, out,
-                        (nc.sync, nc.scalar) if at_the_end else (nc.scalar, nc.scalar),
+                    rotated = keep.tile(
+                        [P, widths[n] // HEAD_DIM, PAIRS, 2], F32, name="rotated_%s%d" % (name, n)
                     )
+                    rotate(nc, rope, rotated, banks[n], tables)
+                    if name == "q":
+                        waiting.append((rotated, out, starts[n]))
+                    else:
+                        at_the_end = n == len(spans) - 1
+                        store((nc.sync, nc.scalar) if at_the_end else (nc.sync, nc.sync), rotated, out, starts[n])

@@ -41,7 +41,7 @@ SCALE_ROWS = 4
 PLANES = 4
 SLOTS = GROUPS // PLANES
 
-WEIGHT_BUFS = 7
+WEIGHT_BUFS = 28
 
 FLOPS = 2 * BATCH * POSITIONS * D_IN * 2 * D_OUT
 
@@ -223,15 +223,15 @@ def tile_optimizedflashattention_pa_k_kernel(
                 ]
                 by_block = words.rearrange("(slot i) p n t -> slot p i (n t)", i=PLANES).bitcast(I32)
                 whole_blocks = SLOTS if name == "q" else SLOTS - 1
-                for slot in range(whole_blocks):
-                    w_block = weights.tile([P, PLANES, D_OUT], U32, align_bytes=64)
-                    nc.sync.dma_start(out=w_block[:].bitcast(I32), in_=by_block[slot])
-                    for i in range(PLANES):
-                        for bank, cols in zip(banks, spans):
-                            multiply_group(
-                                nc, bank, x_codes, x_scales, slot * PLANES + i,
-                                w_block[:, i, cols], planes[SCALE_ROWS * i : P, slot, cols],
-                            )
+                for g in range(whole_blocks * PLANES):
+                    slot, i = divmod(g, PLANES)
+                    w_group = weights.tile([P, D_OUT], U32, align_bytes=64)
+                    nc.sync.dma_start(out=w_group[:].bitcast(I32), in_=by_block[slot][:, i, :])
+                    for bank, cols in zip(banks, spans):
+                        multiply_group(
+                            nc, bank, x_codes, x_scales, g,
+                            w_group[:, cols], planes[SCALE_ROWS * i : P, slot, cols],
+                        )
                 last_parts = []
                 for slot in range(whole_blocks, SLOTS):
                     for n, cols in enumerate(spans):

@@ -95,36 +95,26 @@ def build_rotation_tables(nc, pool):
     nc.vector.tensor_tensor(out=turns[:], in0=turns[:], in1=whole[:], op=ALU.subtract)
     sin_cos = pool.tile([P, 2, PAIRS], F32)
     nc.scalar.activation(out=sin_cos[:], in_=turns[:], func=ACT.Sin, scale=2.0 * math.pi)
-    neg_sin = pool.tile([P, PAIRS], F32)
-    nc.vector.tensor_scalar_mul(out=neg_sin[:], in0=sin_cos[:, 0, :], scalar1=-1.0)
-    return sin_cos[:, 0, :], sin_cos[:, 1, :], neg_sin[:]
+    signed_sin = pool.tile([P, PAIRS, 2], F32)
+    nc.vector.tensor_scalar_mul(out=signed_sin[:, :, 0], in0=sin_cos[:, 0, :], scalar1=-1.0)
+    nc.vector.tensor_copy(out=signed_sin[:, :, 1], in_=sin_cos[:, 0, :])
+    return sin_cos[:, 1, :], signed_sin[:]
 
 
 def rotate(nc, pool, rotated, bank, tables):
-    sin, cos, neg_sin = tables
+    cos, signed_sin = tables
     heads = rotated.shape[1]
     y = bank[:].rearrange("p (h i two) -> p h i two", h=heads, two=2)
-    by_head = [P, heads, PAIRS]
-    direct = pool.tile([P, heads, PAIRS, 2], F32)
+    pairs = [P, heads, PAIRS, 2]
+    crossed = pool.tile(pairs, F32)
     nc.vector.tensor_tensor(
-        out=direct[:],
-        in0=y,
-        in1=cos.unsqueeze(1).unsqueeze(3).to_broadcast([P, heads, PAIRS, 2]),
-        op=ALU.mult,
+        out=crossed[:], in0=y[:, :, :, ::-1], in1=signed_sin.unsqueeze(1).to_broadcast(pairs), op=ALU.mult
     )
-    crossed = pool.tile([P, 2, heads, PAIRS], F32)
+    direct = pool.tile(pairs, F32)
     nc.vector.tensor_tensor(
-        out=crossed[:, 0], in0=y[:, :, :, 1], in1=neg_sin.unsqueeze(1).to_broadcast(by_head), op=ALU.mult
+        out=direct[:], in0=y, in1=cos.unsqueeze(1).unsqueeze(3).to_broadcast(pairs), op=ALU.mult
     )
-    nc.vector.tensor_tensor(
-        out=crossed[:, 1], in0=y[:, :, :, 0], in1=sin.unsqueeze(1).to_broadcast(by_head), op=ALU.mult
-    )
-    nc.vector.tensor_tensor(
-        out=rotated[:],
-        in0=direct[:],
-        in1=crossed[:].rearrange("p two h i -> p h i two"),
-        op=ALU.add,
-    )
+    nc.vector.tensor_tensor(out=rotated[:], in0=direct[:], in1=crossed[:], op=ALU.add)
 
 
 def store(queues, rotated, out, first_col):
@@ -232,23 +222,22 @@ def tile_optimizedflashattention_pa_k_kernel(
                             nc, bank, x_codes, x_scales, g,
                             w_group[:, cols], planes[SCALE_ROWS * i : P, slot, cols],
                         )
-                last_parts = []
-                for slot in range(whole_blocks, SLOTS):
-                    for n, cols in enumerate(spans):
-                        w_part = parts.tile([P, PLANES, widths[n]], U32, name="w_part%d" % n, align_bytes=64)
-                        nc.sync.dma_start(out=w_part[:].bitcast(I32), in_=by_block[slot][:, :, cols])
-                        last_parts.append((slot, w_part))
+                tail = [divmod(g, PLANES) for g in range(whole_blocks * PLANES, GROUPS)]
+                w_parts = {}
+                for n, cols in enumerate(spans):
+                    for slot, i in tail:
+                        w_part = parts.tile([P, widths[n]], U32, name="w_part%d_%d" % (n, i), align_bytes=64)
+                        nc.sync.dma_start(out=w_part[:].bitcast(I32), in_=by_block[slot][:, i, cols])
+                        w_parts[n, i] = w_part
                 if name == "k":
                     for rotated, q_out, first_col in waiting:
                         store((nc.sync, nc.sync), rotated, q_out, first_col)
                 for n, cols in enumerate(spans):
-                    if last_parts:
-                        slot, w_part = last_parts[n]
-                        for i in range(PLANES):
-                            multiply_group(
-                                nc, banks[n], x_codes, x_scales, slot * PLANES + i,
-                                w_part[:, i, :], planes[SCALE_ROWS * i : P, slot, cols],
-                            )
+                    for slot, i in tail:
+                        multiply_group(
+                            nc, banks[n], x_codes, x_scales, slot * PLANES + i,
+                            w_parts[n, i][:], planes[SCALE_ROWS * i : P, slot, cols],
+                        )
                     rotated = keep.tile(
                         [P, widths[n] // HEAD_DIM, PAIRS, 2], F32, name="rotated_%s%d" % (name, n)
                     )

import math
from contextlib import ExitStack

import concourse.mybir as mybir
from concourse.masks import make_identity

F32 = mybir.dt.float32
BF16 = mybir.dt.bfloat16
I32 = mybir.dt.int32
U32 = mybir.dt.uint32
U8 = mybir.dt.uint8
FP8X4 = mybir.dt.float8_e4m3fn_x4
ALU = mybir.AluOpType
ACT = mybir.ActivationFunctionType

P = 128
PACK = 4
K_PASS = P * PACK

BATCH, POSITIONS, D_IN = 2, 64, 16384
HEADS, HEAD_DIM = 16, 64
PAIRS = HEAD_DIM // 2
DOUBLINGS = 5
assert 2**DOUBLINGS == PAIRS
D_OUT = HEADS * HEAD_DIM
ROPE_BASE = 10000.0

GROUPS = D_IN // K_PASS
BANK_COLS = 512

TILE_COLS = {"q": (512, 512), "k": (512, 256, 256)}
TILE_BANKS = {"q": (0, 1), "k": (2, 3, 4)}

X_CHUNKS = 4
CHUNK_GROUPS = GROUPS // X_CHUNKS
BANK_GROUPS = 2

QUADRANT = 32
QUADRANTS = P // QUADRANT
SCALE_ROWS = 4
PLANES = 4
SLOTS = GROUPS // PLANES

WEIGHT_BUFS = 28

FLOPS = 2 * BATCH * POSITIONS * D_IN * 2 * D_OUT


def load_scale_planes(nc, planes, scales):
    by_row = scales.bitcast(F32).rearrange("(slot i) q n -> q i slot n", i=PLANES)
    for r in range(SCALE_ROWS):
        for quadrant in range(QUADRANTS):
            first = QUADRANT * quadrant + r
            nc.gpsimd.dma_start(
                out=planes[first : first + PLANES * SCALE_ROWS : SCALE_ROWS, :, :].bitcast(F32),
                in_=by_row[SCALE_ROWS * quadrant + r],
            )


def build_rotation_tables(nc, pool):
    pos_int = pool.tile([P, 1], I32)
    nc.gpsimd.iota(pos_int[:], pattern=[[1, 1]], base=0, channel_multiplier=1)
    nc.vector.tensor_single_scalar(
        out=pos_int[:], in_=pos_int[:], scalar=POSITIONS - 1, op=ALU.bitwise_and
    )
    pos_turns = pool.tile([P, 1], F32)
    nc.vector.tensor_copy(out=pos_turns[:], in_=pos_int[:])
    nc.vector.tensor_scalar_mul(out=pos_turns[:], in0=pos_turns[:], scalar1=1.0 / (2.0 * math.pi))

    ratio = ROPE_BASE ** (-2.0 / HEAD_DIM)
    inv_freq = pool.tile([P, PAIRS], F32)
    nc.vector.memset(inv_freq[:, 0:1], 1.0)
    for doubling in range(DOUBLINGS):
        length = 2**doubling
        nc.vector.tensor_scalar_mul(
            out=inv_freq[:, length : 2 * length], in0=inv_freq[:, 0:length], scalar1=ratio**length
        )

    turns = pool.tile([P, 2, PAIRS], F32)
    for row, phase in enumerate((0.0, 0.25)):
        nc.vector.tensor_scalar(
            out=turns[:, row, :],
            in0=inv_freq[:],
            scalar1=pos_turns[:, 0:1],
            scalar2=phase,
            op0=ALU.mult,
            op1=ALU.add,
        )
    whole_int = pool.tile([P, 2, PAIRS], I32)
    nc.vector.tensor_copy(out=whole_int[:], in_=turns[:])
    whole = pool.tile([P, 2, PAIRS], F32)
    nc.vector.tensor_copy(out=whole[:], in_=whole_int[:])
    nc.vector.tensor_tensor(out=turns[:], in0=turns[:], in1=whole[:], op=ALU.subtract)
    nc.vector.tensor_single_scalar(out=whole[:], in_=turns[:], scalar=0.5, op=ALU.is_gt)
    nc.vector.tensor_tensor(out=turns[:], in0=turns[:], in1=whole[:], op=ALU.subtract)
    sin_cos = pool.tile([P, 2, PAIRS], F32)
    nc.scalar.activation(out=sin_cos[:], in_=turns[:], func=ACT.Sin, scale=2.0 * math.pi)
    signed_sin = pool.tile([P, PAIRS, 2], F32)
    nc.vector.tensor_scalar_mul(out=signed_sin[:, :, 0], in0=sin_cos[:, 0, :], scalar1=-1.0)
    nc.vector.tensor_copy(out=signed_sin[:, :, 1], in_=sin_cos[:, 0, :])
    return sin_cos[:, 1, :], signed_sin[:]


def rotate(nc, pool, rotated, bank, tables):
    cos, signed_sin = tables
    heads = rotated.shape[1]
    y = bank[:].rearrange("p (h i two) -> p h i two", h=heads, two=2)
    pairs = [P, heads, PAIRS, 2]
    crossed = pool.tile(pairs, F32)
    nc.vector.tensor_tensor(
        out=crossed[:], in0=y[:, :, :, ::-1], in1=signed_sin.unsqueeze(1).to_broadcast(pairs), op=ALU.mult
    )
    direct = pool.tile(pairs, F32)
    nc.vector.tensor_tensor(
        out=direct[:], in0=y, in1=cos.unsqueeze(1).unsqueeze(3).to_broadcast(pairs), op=ALU.mult
    )
    nc.vector.tensor_tensor(out=rotated[:], in0=direct[:], in1=crossed[:], op=ALU.add)


def store(queues, rotated, out, first_col):
    heads = rotated.shape[1]
    first_head = first_col // HEAD_DIM
    for b in range(BATCH):
        queues[b].dma_start(
            out=out[b, first_head : first_head + heads].rearrange("h s d -> s h d"),
            in_=rotated[b * POSITIONS : (b + 1) * POSITIONS].rearrange("p h i two -> p h (i two)"),
        )


def multiply_group(nc, bank, x_codes, x_scales, g, w_codes, w_scales):
    nc.tensor.matmul_mx(
        out=bank[:],
        lhsT=x_codes[:, g, :].bitcast(FP8X4),
        lhsT_scale=x_scales[:, g, :],
        rhs=w_codes.bitcast(FP8X4),
        rhs_scale=w_scales,
        start=(g == 0),
        stop=(g == GROUPS - 1),
    )


def tile_optimizedflashattention_pa_k_kernel(
    tc, x, w_q_words, w_q_scales, w_k_words, w_k_scales, out_q, out_k
):
    nc = tc.nc
    with ExitStack() as ctx:
        keep = ctx.enter_context(tc.tile_pool(name="keep", bufs=1))
        stage = ctx.enter_context(tc.tile_pool(name="stage", bufs=3))
        weights = ctx.enter_context(tc.tile_pool(name="weights", bufs=WEIGHT_BUFS))
        parts = ctx.enter_context(tc.tile_pool(name="parts", bufs=1))
        rope = ctx.enter_context(tc.tile_pool(name="rope", bufs=2))
        flipped = ctx.enter_context(tc.psum_pool(name="flipped", bufs=3))
        sums = ctx.enter_context(tc.psum_pool(name="sums", bufs=1))

        x_rows = x.rearrange("b s d -> (b s) d")
        chunk_cols = CHUNK_GROUPS * K_PASS
        x_chunks = []
        for c in range(X_CHUNKS):
            x_chunk = keep.tile([P, chunk_cols], BF16, name="x_chunk%d" % c)
            nc.sync.dma_start(out=x_chunk[:], in_=x_rows[:, c * chunk_cols : (c + 1) * chunk_cols])
            x_chunks.append(x_chunk)

        identity = keep.tile([P, P], F32)
        make_identity(nc, identity[:])
        projections = []
        for name, words, scales, out in (
            ("q", w_q_words, w_q_scales, out_q),
            ("k", w_k_words, w_k_scales, out_k),
        ):
            planes = keep.tile([P, SLOTS, D_OUT], U8, name="planes_%s" % name, align_bytes=64)
            nc.vector.memset(planes[:].rearrange("p slot n -> p (slot n)").bitcast(I32), 0)
            load_scale_planes(nc, planes, scales)
            projections.append((name, words, planes, out))

        x_codes = keep.tile([P, GROUPS, P], U32, align_bytes=64)
        x_scales = keep.tile([P, GROUPS, P], U8, align_bytes=64)
        words_per_group = K_PASS // 2
        for c in range(X_CHUNKS):
            x_words = x_chunks[c][:].bitcast(F32)
            for first in range(0, CHUNK_GROUPS, BANK_GROUPS):
                x_t = flipped.tile([P, BANK_GROUPS, 2, P], F32)
                for j in range(BANK_GROUPS):
                    start_word = (first + j) * words_per_group
                    for u in range(2):
                        nc.tensor.transpose(
                            x_t[:, j, u, :],
                            x_words[:, start_word + u : start_word + words_per_group : 2],
                            identity[:],
                        )
                grouped = stage.tile([P, BANK_GROUPS, P, PACK], BF16, align_bytes=64)
                nc.scalar.copy(
                    out=grouped[:].bitcast(F32), in_=x_t[:].rearrange("p j u token -> p j token u")
                )
                g = c * CHUNK_GROUPS + first
                nc.vector.quantize_mx(
                    out=x_codes[:, g : g + BANK_GROUPS, :]
                    .rearrange("p j token -> p (j token)")
                    .bitcast(FP8X4),
                    scales=x_scales[:, g : g + BANK_GROUPS, :].rearrange("p j token -> p (j token)"),
                    in_=grouped[:].rearrange("p j token t -> p (j token t)"),
                )

        tables = build_rotation_tables(nc, keep)

        with tc.manual_schedule(engines={mybir.EngineType.SP, mybir.EngineType.PE}):
            waiting = []
            for name, words, planes, out in projections:
                widths = TILE_COLS[name]
                starts = [sum(widths[:n]) for n in range(len(widths))]
                spans = [slice(first, first + width) for first, width in zip(starts, widths)]
                banks = [
                    sums.tile([P, width], F32, name="sum%d" % b) for width, b in zip(widths, TILE_BANKS[name])
                ]
                by_block = words.rearrange("(slot i) p n t -> slot p i (n t)", i=PLANES).bitcast(I32)
                whole_blocks = SLOTS if name == "q" else SLOTS - 1
                for g in range(whole_blocks * PLANES):
                    slot, i = divmod(g, PLANES)
                    w_group = weights.tile([P, D_OUT], U32, align_bytes=64)
                    nc.sync.dma_start(out=w_group[:].bitcast(I32), in_=by_block[slot][:, i, :])
                    for bank, cols in zip(banks, spans):
                        multiply_group(
                            nc, bank, x_codes, x_scales, g,
                            w_group[:, cols], planes[SCALE_ROWS * i : P, slot, cols],
                        )
                tail = [divmod(g, PLANES) for g in range(whole_blocks * PLANES, GROUPS)]
                w_parts = {}
                for n, cols in enumerate(spans):
                    for slot, i in tail:
                        w_part = parts.tile([P, widths[n]], U32, name="w_part%d_%d" % (n, i), align_bytes=64)
                        nc.sync.dma_start(out=w_part[:].bitcast(I32), in_=by_block[slot][:, i, cols])
                        w_parts[n, i] = w_part
                if name == "k":
                    for rotated, q_out, first_col in waiting:
                        store((nc.sync, nc.sync), rotated, q_out, first_col)
                for n, cols in enumerate(spans):
                    for slot, i in tail:
                        multiply_group(
                            nc, banks[n], x_codes, x_scales, slot * PLANES + i,
                            w_parts[n, i][:], planes[SCALE_ROWS * i : P, slot, cols],
                        )
                    rotated = keep.tile(
                        [P, widths[n] // HEAD_DIM, PAIRS, 2], F32, name="rotated_%s%d" % (name, n)
                    )
                    rotate(nc, rope, rotated, banks[n], tables)
                    if name == "q":
                        waiting.append((rotated, out, starts[n]))
                    else:
                        at_the_end = n == len(spans) - 1
                        store((nc.sync, nc.scalar) if at_the_end else (nc.sync, nc.sync), rotated, out, starts[n])
